import numpy as np
import ml_dtypes


def mxq(x, axis, fmt="e4m3"):
    dtype, down = {"e4m3": (ml_dtypes.float8_e4m3fn, 7), "e5m2": (ml_dtypes.float8_e5m2, 14)}[fmt]
    v = np.moveaxis(np.asarray(x, np.float32).astype(ml_dtypes.bfloat16).astype(np.float64), axis, -1)
    blocks = v.reshape(v.shape[:-1] + (-1, 32))
    amax = np.abs(blocks).max(-1, keepdims=True)
    byte = np.maximum(np.where(amax > 0, np.frexp(amax)[1] - 1 + 127, 0) - down, 1)
    scale = np.exp2(byte - 127.0)
    codes = (blocks / scale).astype(np.float32).astype(dtype).astype(np.float64)
    return np.moveaxis((codes * scale).reshape(v.shape), -1, axis)


WIDE = False


def mx_kscale(k):
    if not WIDE:
        return np.ones(k)
    levels = np.array([10, -10, 5, -5, 0])
    a = np.random.permutation(np.resize(levels, k // 512 * 4)).reshape(k // 512, 4)
    idx = np.arange(k)
    return np.exp2(a[idx // 512, idx % 128 // 32])


BF16 = ml_dtypes.bfloat16


def bf(x):
    return np.asarray(x, np.float32).astype(BF16)


def f64(x):
    return np.asarray(x).astype(np.float64)


B, S, D, H, HD = 4, 128, 1536, 16, 96
DPA = HD // 6


def build_rope_freqs():
    return 1.0 / (10000.0 ** (np.arange(DPA) / DPA))


def apply_rope_3d(t, coords, freqs):
    theta = (coords[..., None] * freqs).reshape(*coords.shape[:-1], -1)[:, None]
    cos, sin = np.cos(theta), np.sin(theta)
    tp = t.reshape(*t.shape[:-1], t.shape[-1] // 2, 2)
    t1, t2 = tp[..., 0], tp[..., 1]
    out = np.stack([t1 * cos - t2 * sin, t1 * sin + t2 * cos], axis=-1)
    return out.reshape(t.shape)


def setup_inputs():
    s = mx_kscale(D)
    return {'x': bf(np.random.standard_normal((B, S, D)) * s),
            'coords': bf(np.random.standard_normal((B, S, 3))),
            'W_qkv': bf(np.random.standard_normal((3 * H * HD, D)) / np.sqrt(D) / s)}


def reference(x, coords, W_qkv):
    freqs = build_rope_freqs()
    c = f64(coords)
    qkv = mxq(f64(x), 2, 'e4m3') @ mxq(f64(W_qkv), 1, 'e4m3').T
    qkv = qkv.reshape(B, S, 3, H, HD)
    q, k, v = (qkv[:, :, i].transpose(0, 2, 1, 3) for i in range(3))
    return apply_rope_3d(q, c, freqs), apply_rope_3d(k, c, freqs), v

@@ -1,0 +1,200 @@
+import math
+from contextlib import ExitStack
+
+import concourse.mybir as mybir
+from concourse.masks import make_identity
+
+F32 = mybir.dt.float32
+BF16 = mybir.dt.bfloat16
+U32 = mybir.dt.uint32
+U8 = mybir.dt.uint8
+FP8X4 = mybir.dt.float8_e4m3fn_x4
+ALU = mybir.AluOpType
+ACT = mybir.ActivationFunctionType
+
+P = 128
+BATCH = 4
+FEATURES = 1536
+HEADS = 16
+HEAD_DIM = 96
+PAIRS = HEAD_DIM // 2
+FREQS = HEAD_DIM // 6
+K_PASS = 512
+PASSES = FEATURES // K_PASS
+PASS_WORDS = K_PASS // 2
+
+GROUP_HEADS = 4
+GROUP_COLS = GROUP_HEADS * HEAD_DIM
+GROUP_TILES = GROUP_COLS // P
+GROUPS_PER_OUTPUT = HEADS // GROUP_HEADS
+PARTS = ((0, 2 * P), (2 * P, GROUP_COLS))
+
+FLOPS = 2 * BATCH * P * FEATURES * 3 * HEADS * HEAD_DIM
+
+TURN_HI = 6.28125
+TURN_MID = 4059.0 / 2097152.0
+TURN_LO = 2.0 * math.pi - TURN_HI - TURN_MID
+ROUND_MAGIC = 12582912.0
+PI_BELOW = 3.1415925
+
+
+def rotation_table(nc, const, coords):
+    coords_sb = const.tile([P, BATCH, 3], BF16)
+    nc.scalar.dma_start(out=coords_sb[:], in_=coords.rearrange("b s a -> s b a"))
+
+    theta = const.tile([P, BATCH, PAIRS], F32)
+    theta_by_freq = theta[:].rearrange("s b (a j) -> s (b a) j", j=FREQS)
+    for j in range(FREQS):
+        nc.vector.tensor_scalar(
+            out=theta_by_freq[:, :, j],
+            in0=coords_sb[:].rearrange("s b a -> s (b a)"),
+            scalar1=10000.0 ** (-j / FREQS),
+            scalar2=None,
+            op0=ALU.mult,
+        )
+
+    turns = const.tile([P, BATCH, PAIRS], F32)
+    nc.vector.tensor_scalar(
+        out=turns[:], in0=theta[:], scalar1=0.5 / math.pi, scalar2=ROUND_MAGIC, op0=ALU.mult, op1=ALU.add
+    )
+    nc.vector.tensor_scalar(out=turns[:], in0=turns[:], scalar1=ROUND_MAGIC, scalar2=None, op0=ALU.subtract)
+    reduced = const.tile([P, BATCH, PAIRS], F32)
+    nc.vector.scalar_tensor_tensor(
+        out=reduced[:], in0=turns[:], scalar=-TURN_HI, in1=theta[:], op0=ALU.mult, op1=ALU.add
+    )
+    for piece in (TURN_MID, TURN_LO):
+        nc.vector.scalar_tensor_tensor(
+            out=reduced[:], in0=turns[:], scalar=-piece, in1=reduced[:], op0=ALU.mult, op1=ALU.add
+        )
+    nc.vector.tensor_scalar(
+        out=reduced[:], in0=reduced[:], scalar1=-PI_BELOW, scalar2=PI_BELOW, op0=ALU.max, op1=ALU.min
+    )
+    magnitude = const.tile([P, BATCH, PAIRS], F32)
+    nc.vector.scalar_tensor_tensor(
+        out=magnitude[:], in0=reduced[:], scalar=-1.0, in1=reduced[:], op0=ALU.mult, op1=ALU.max
+    )
+
+    angle = const.tile([P, BATCH, PAIRS, 2, 2], F32)
+    for i in range(2):
+        nc.vector.tensor_scalar(
+            out=angle[:, :, :, i, i], in0=magnitude[:], scalar1=-1.0, scalar2=0.5 * math.pi,
+            op0=ALU.mult, op1=ALU.add,
+        )
+    nc.vector.tensor_copy(out=angle[:, :, :, 0, 1], in_=reduced[:])
+    nc.vector.tensor_scalar(out=angle[:, :, :, 1, 0], in0=reduced[:], scalar1=-1.0, scalar2=None, op0=ALU.mult)
+    rot = const.tile([P, BATCH, PAIRS, 2, 2], F32)
+    nc.scalar.activation(out=rot[:], in_=angle[:], func=ACT.Sin)
+    return rot
+
+
+def quantise_rows(nc, flip_psum, stage, identity, row_tiles, g, codes, scales):
+    cols = P * len(row_tiles)
+    flipped = flip_psum.tile([P, 2, cols], F32, tag="flipped")
+    for u in range(2):
+        first = PASS_WORDS * g + P * u
+        for t, rows in enumerate(row_tiles):
+            nc.tensor.transpose(flipped[:, u, P * t : P * t + P], rows[:, first : first + P], identity[:])
+    grouped = stage.tile([P, 4 * cols], BF16, tag="grouped", align_bytes=64)
+    nc.scalar.copy(
+        out=grouped[:].bitcast(F32).rearrange("q (c u) -> q c u", u=2),
+        in_=flipped[:].rearrange("q u c -> q c u"),
+    )
+    nc.vector.quantize_mx(out=codes.bitcast(FP8X4), scales=scales, in_=grouped[:])
+
+
+def tile_ropeattention_pa_kernel(tc, x, coords, W_qkv, out_0, out_1, out_2):
+    nc = tc.nc
+    outputs = (out_0, out_1, out_2)
+    groups = [(which, quarter) for quarter in range(GROUPS_PER_OUTPUT) for which in range(3)]
+
+    with ExitStack() as ctx:
+        const = ctx.enter_context(tc.tile_pool(name="const", bufs=1))
+        weights = ctx.enter_context(tc.tile_pool(name="weights", bufs=len(groups)))
+        stage = ctx.enter_context(tc.tile_pool(name="stage", bufs=6))
+        packed = ctx.enter_context(tc.tile_pool(name="packed", bufs=3))
+        work = ctx.enter_context(tc.tile_pool(name="work", bufs=3))
+        results = ctx.enter_context(tc.tile_pool(name="results", bufs=24))
+        flip_psum = ctx.enter_context(tc.psum_pool(name="flip_psum", bufs=4))
+        acc_psum = ctx.enter_context(tc.psum_pool(name="acc_psum", bufs=4))
+
+        x_raw = const.tile([P, BATCH, FEATURES], BF16)
+        for b in range(BATCH):
+            nc.sync.dma_start(out=x_raw[:, b, :], in_=x[b])
+        w_raw = []
+        for which, quarter in groups:
+            first_row = which * HEADS * HEAD_DIM + quarter * GROUP_COLS
+            w_rows = weights.tile([P, GROUP_TILES, FEATURES], BF16, tag="w_rows")
+            nc.sync.dma_start(
+                out=w_rows[:],
+                in_=W_qkv[first_row : first_row + GROUP_COLS, :].rearrange("(t p) k -> p t k", p=P),
+            )
+            w_raw.append(w_rows)
+
+        identity = const.tile([P, P], F32)
+        make_identity(nc, identity[:])
+        rot = rotation_table(nc, const, coords)
+
+        x_codes = const.tile([P, PASSES, BATCH * P], U32, align_bytes=64)
+        x_scales = const.tile([P, PASSES, BATCH * P], U8, align_bytes=64)
+        x_words = x_raw[:].bitcast(F32)
+        for b in range(0, BATCH, 2):
+            for g in range(PASSES):
+                quantise_rows(
+                    nc, flip_psum, stage, identity, [x_words[:, b, :], x_words[:, b + 1, :]], g,
+                    x_codes[:, g, P * b : P * b + 2 * P], x_scales[:, g, P * b : P * b + 2 * P],
+                )
+
+        def prepare(i):
+            w_words = w_raw[i][:].bitcast(F32)
+            w_codes = packed.tile([P, PASSES, GROUP_COLS], U32, tag="w_codes", align_bytes=64)
+            w_scales = packed.tile([P, PASSES, GROUP_COLS], U8, tag="w_scales", align_bytes=64)
+            for g in range(PASSES):
+                for lo, hi in PARTS:
+                    quantise_rows(
+                        nc, flip_psum, stage, identity,
+                        [w_words[:, t, :] for t in range(lo // P, hi // P)], g,
+                        w_codes[:, g, lo:hi], w_scales[:, g, lo:hi],
+                    )
+            return w_codes, w_scales
+
+        def project(i, w_codes, w_scales):
+            which, quarter = groups[i]
+            for b in range(BATCH):
+                acc = acc_psum.tile([P, GROUP_COLS], F32, tag="acc")
+                for lo, hi in PARTS:
+                    for g in range(PASSES):
+                        nc.tensor.matmul_mx(
+                            out=acc[:, lo:hi],
+                            lhsT=x_codes[:, g, P * b : P * b + P].bitcast(FP8X4),
+                            lhsT_scale=x_scales[:, g, P * b : P * b + P],
+                            rhs=w_codes[:, g, lo:hi].bitcast(FP8X4),
+                            rhs_scale=w_scales[:, g, lo:hi],
+                            start=(g == 0),
+                            stop=(g == PASSES - 1),
+                        )
+                result = results.tile([P, GROUP_HEADS, PAIRS, 2], F32, tag="result")
+                if which == 2:
+                    nc.scalar.copy(out=result[:].rearrange("s h n e -> s (h n e)"), in_=acc[:])
+                else:
+                    shape = [P, GROUP_HEADS, PAIRS, 2, 2]
+                    products = work.tile(shape, F32, tag="products")
+                    nc.vector.tensor_tensor(
+                        out=products[:],
+                        in0=acc[:].rearrange("s (h n w) -> s h n w", h=GROUP_HEADS, w=2).unsqueeze(4).to_broadcast(shape),
+                        in1=rot[:, b].unsqueeze(1).to_broadcast(shape),
+                        op=ALU.mult,
+                    )
+                    nc.vector.tensor_tensor(
+                        out=result[:], in0=products[:, :, :, 0, :], in1=products[:, :, :, 1, :], op=ALU.add
+                    )
+                first_head = quarter * GROUP_HEADS
+                nc.sync.dma_start(
+                    out=outputs[which][b, first_head : first_head + GROUP_HEADS].rearrange("h s d -> s h d"),
+                    in_=result[:].rearrange("s h n e -> s h (n e)"),
+                )
+
+        ready = prepare(0)
+        for i in range(len(groups)):
+            following = prepare(i + 1) if i + 1 < len(groups) else None
+            project(i, ready[0], ready[1])
+            ready = following

@@ -38,10 +38,7 @@ ROUND_MAGIC = 12582912.0
 PI_BELOW = 3.1415925
 
 
-def rotation_table(nc, const, coords):
-    coords_sb = const.tile([P, BATCH, 3], BF16)
-    nc.scalar.dma_start(out=coords_sb[:], in_=coords.rearrange("b s a -> s b a"))
-
+def rotation_arguments(nc, const, coords_sb):
     theta = const.tile([P, BATCH, PAIRS], F32)
     theta_by_freq = theta[:].rearrange("s b (a j) -> s (b a) j", j=FREQS)
     for j in range(FREQS):
@@ -82,12 +79,10 @@ def rotation_table(nc, const, coords):
         )
     nc.vector.tensor_copy(out=angle[:, :, :, 0, 1], in_=reduced[:])
     nc.vector.tensor_scalar(out=angle[:, :, :, 1, 0], in0=reduced[:], scalar1=-1.0, scalar2=None, op0=ALU.mult)
-    rot = const.tile([P, BATCH, PAIRS, 2, 2], F32)
-    nc.scalar.activation(out=rot[:], in_=angle[:], func=ACT.Sin)
-    return rot
+    return angle
 
 
-def quantise_rows(nc, flip_psum, stage, identity, row_tiles, g, codes, scales):
+def flip_rows(nc, flip_psum, stage, identity, row_tiles, g):
     cols = P * len(row_tiles)
     flipped = flip_psum.tile([P, 2, cols], F32, tag="flipped")
     for u in range(2):
@@ -99,13 +94,15 @@ def quantise_rows(nc, flip_psum, stage, identity, row_tiles, g, codes, scales):
         out=grouped[:].bitcast(F32).rearrange("q (c u) -> q c u", u=2),
         in_=flipped[:].rearrange("q u c -> q c u"),
     )
-    nc.vector.quantize_mx(out=codes.bitcast(FP8X4), scales=scales, in_=grouped[:])
+    return grouped
 
 
 def tile_ropeattention_pa_kernel(tc, x, coords, W_qkv, out_0, out_1, out_2):
     nc = tc.nc
     outputs = (out_0, out_1, out_2)
     groups = [(which, quarter) for quarter in range(GROUPS_PER_OUTPUT) for which in range(3)]
+    pieces = [(g, lo, hi) for g in range(PASSES) for lo, hi in PARTS]
+    halves = (pieces[:3], pieces[3:])
 
     with ExitStack() as ctx:
         const = ctx.enter_context(tc.tile_pool(name="const", bufs=1))
@@ -116,7 +113,10 @@ def tile_ropeattention_pa_kernel(tc, x, coords, W_qkv, out_0, out_1, out_2):
         results = ctx.enter_context(tc.tile_pool(name="results", bufs=24))
         flip_psum = ctx.enter_context(tc.psum_pool(name="flip_psum", bufs=4))
         acc_psum = ctx.enter_context(tc.psum_pool(name="acc_psum", bufs=4))
+        ctx.enter_context(tc.manual_schedule())
 
+        coords_sb = const.tile([P, BATCH, 3], BF16)
+        nc.scalar.dma_start(out=coords_sb[:], in_=coords.rearrange("b s a -> s b a"))
         x_raw = const.tile([P, BATCH, FEATURES], BF16)
         for b in range(BATCH):
             nc.sync.dma_start(out=x_raw[:, b, :], in_=x[b])
@@ -130,71 +130,99 @@ def tile_ropeattention_pa_kernel(tc, x, coords, W_qkv, out_0, out_1, out_2):
             )
             w_raw.append(w_rows)
 
+        warm = const.tile([P, 1], F32)
+        nc.vector.memset(warm[:], 0.0)
+        nc.scalar.activation(out=warm[:], in_=warm[:], func=ACT.Sin)
+
         identity = const.tile([P, P], F32)
         make_identity(nc, identity[:])
-        rot = rotation_table(nc, const, coords)
+        angle = rotation_arguments(nc, const, coords_sb)
 
         x_codes = const.tile([P, PASSES, BATCH * P], U32, align_bytes=64)
         x_scales = const.tile([P, PASSES, BATCH * P], U8, align_bytes=64)
         x_words = x_raw[:].bitcast(F32)
         for b in range(0, BATCH, 2):
+            flipped_x = [
+                flip_rows(nc, flip_psum, stage, identity, [x_words[:, b, :], x_words[:, b + 1, :]], g)
+                for g in range(PASSES)
+            ]
             for g in range(PASSES):
-                quantise_rows(
-                    nc, flip_psum, stage, identity, [x_words[:, b, :], x_words[:, b + 1, :]], g,
-                    x_codes[:, g, P * b : P * b + 2 * P], x_scales[:, g, P * b : P * b + 2 * P],
+                nc.vector.quantize_mx(
+                    out=x_codes[:, g, P * b : P * b + 2 * P].bitcast(FP8X4),
+                    scales=x_scales[:, g, P * b : P * b + 2 * P],
+                    in_=flipped_x[g][:],
                 )
 
-        def prepare(i):
+        def flip_half(i, half):
             w_words = w_raw[i][:].bitcast(F32)
+            return [
+                flip_rows(nc, flip_psum, stage, identity, [w_words[:, t, :] for t in range(lo // P, hi // P)], g)
+                for g, lo, hi in halves[half]
+            ]
+
+        def quantise_half(half, flipped_w, w_codes, w_scales):
+            for (g, lo, hi), grouped in zip(halves[half], flipped_w):
+                nc.vector.quantize_mx(
+                    out=w_codes[:, g, lo:hi].bitcast(FP8X4), scales=w_scales[:, g, lo:hi], in_=grouped[:]
+                )
+
+        def multiply(b, w_codes, w_scales):
+            acc = acc_psum.tile([P, GROUP_COLS], F32, tag="acc")
+            for lo, hi in PARTS:
+                for g in range(PASSES):
+                    nc.tensor.matmul_mx(
+                        out=acc[:, lo:hi],
+                        lhsT=x_codes[:, g, P * b : P * b + P].bitcast(FP8X4),
+                        lhsT_scale=x_scales[:, g, P * b : P * b + P],
+                        rhs=w_codes[:, g, lo:hi].bitcast(FP8X4),
+                        rhs_scale=w_scales[:, g, lo:hi],
+                        start=(g == 0),
+                        stop=(g == PASSES - 1),
+                    )
+            return acc
+
+        def finish(i, b, acc):
+            which, quarter = groups[i]
+            result = results.tile([P, GROUP_HEADS, PAIRS, 2], F32, tag="result")
+            if which == 2:
+                nc.scalar.copy(out=result[:].rearrange("s h n e -> s (h n e)"), in_=acc[:])
+            else:
+                shape = [P, GROUP_HEADS, PAIRS, 2, 2]
+                products = work.tile(shape, F32, tag="products")
+                nc.vector.tensor_tensor(
+                    out=products[:],
+                    in0=acc[:].rearrange("s (h n w) -> s h n w", h=GROUP_HEADS, w=2).unsqueeze(4).to_broadcast(shape),
+                    in1=rot[:, b].unsqueeze(1).to_broadcast(shape),
+                    op=ALU.mult,
+                )
+                nc.vector.tensor_tensor(
+                    out=result[:], in0=products[:, :, :, 0, :], in1=products[:, :, :, 1, :], op=ALU.add
+                )
+            first_head = quarter * GROUP_HEADS
+            nc.sync.dma_start(
+                out=outputs[which][b, first_head : first_head + GROUP_HEADS].rearrange("h s d -> s h d"),
+                in_=result[:].rearrange("s h n e -> s h (n e)"),
+            )
+
+        def new_operand():
             w_codes = packed.tile([P, PASSES, GROUP_COLS], U32, tag="w_codes", align_bytes=64)
             w_scales = packed.tile([P, PASSES, GROUP_COLS], U8, tag="w_scales", align_bytes=64)
-            for g in range(PASSES):
-                for lo, hi in PARTS:
-                    quantise_rows(
-                        nc, flip_psum, stage, identity,
-                        [w_words[:, t, :] for t in range(lo // P, hi // P)], g,
-                        w_codes[:, g, lo:hi], w_scales[:, g, lo:hi],
-                    )
             return w_codes, w_scales
 
-        def project(i, w_codes, w_scales):
-            which, quarter = groups[i]
-            for b in range(BATCH):
-                acc = acc_psum.tile([P, GROUP_COLS], F32, tag="acc")
-                for lo, hi in PARTS:
-                    for g in range(PASSES):
-                        nc.tensor.matmul_mx(
-                            out=acc[:, lo:hi],
-                            lhsT=x_codes[:, g, P * b : P * b + P].bitcast(FP8X4),
-                            lhsT_scale=x_scales[:, g, P * b : P * b + P],
-                            rhs=w_codes[:, g, lo:hi].bitcast(FP8X4),
-                            rhs_scale=w_scales[:, g, lo:hi],
-                            start=(g == 0),
-                            stop=(g == PASSES - 1),
-                        )
-                result = results.tile([P, GROUP_HEADS, PAIRS, 2], F32, tag="result")
-                if which == 2:
-                    nc.scalar.copy(out=result[:].rearrange("s h n e -> s (h n e)"), in_=acc[:])
-                else:
-                    shape = [P, GROUP_HEADS, PAIRS, 2, 2]
-                    products = work.tile(shape, F32, tag="products")
-                    nc.vector.tensor_tensor(
-                        out=products[:],
-                        in0=acc[:].rearrange("s (h n w) -> s h n w", h=GROUP_HEADS, w=2).unsqueeze(4).to_broadcast(shape),
-                        in1=rot[:, b].unsqueeze(1).to_broadcast(shape),
-                        op=ALU.mult,
-                    )
-                    nc.vector.tensor_tensor(
-                        out=result[:], in0=products[:, :, :, 0, :], in1=products[:, :, :, 1, :], op=ALU.add
-                    )
-                first_head = quarter * GROUP_HEADS
-                nc.sync.dma_start(
-                    out=outputs[which][b, first_head : first_head + GROUP_HEADS].rearrange("h s d -> s h d"),
-                    in_=result[:].rearrange("s h n e -> s h (n e)"),
-                )
+        ready = new_operand()
+        for half in range(2):
+            quantise_half(half, flip_half(0, half), ready[0], ready[1])
+        rot = const.tile([P, BATCH, PAIRS, 2, 2], F32)
+        nc.scalar.activation(out=rot[:], in_=angle[:], func=ACT.Sin)
 
-        ready = prepare(0)
         for i in range(len(groups)):
-            following = prepare(i + 1) if i + 1 < len(groups) else None
-            project(i, ready[0], ready[1])
+            last = i + 1 == len(groups)
+            following = None if last else new_operand()
+            for half in range(2):
+                flipped_w = None if last else flip_half(i + 1, half)
+                accs = [multiply(b, ready[0], ready[1]) for b in (2 * half, 2 * half + 1)]
+                finish(i, 2 * half, accs[0])
+                if not last:
+                    quantise_half(half, flipped_w, following[0], following[1])
+                finish(i, 2 * half + 1, accs[1])
             ready = following

@@ -106,11 +106,11 @@ def tile_ropeattention_pa_kernel(tc, x, coords, W_qkv, out_0, out_1, out_2):
 
     with ExitStack() as ctx:
         const = ctx.enter_context(tc.tile_pool(name="const", bufs=1))
-        weights = ctx.enter_context(tc.tile_pool(name="weights", bufs=len(groups)))
+        weights = ctx.enter_context(tc.tile_pool(name="weights", bufs=9))
         stage = ctx.enter_context(tc.tile_pool(name="stage", bufs=6))
         packed = ctx.enter_context(tc.tile_pool(name="packed", bufs=3))
-        work = ctx.enter_context(tc.tile_pool(name="work", bufs=3))
-        results = ctx.enter_context(tc.tile_pool(name="results", bufs=24))
+        work = ctx.enter_context(tc.tile_pool(name="work", bufs=4))
+        results = ctx.enter_context(tc.tile_pool(name="results", bufs=40))
         flip_psum = ctx.enter_context(tc.psum_pool(name="flip_psum", bufs=4))
         acc_psum = ctx.enter_context(tc.psum_pool(name="acc_psum", bufs=4))
         ctx.enter_context(tc.manual_schedule())
@@ -181,27 +181,23 @@ def tile_ropeattention_pa_kernel(tc, x, coords, W_qkv, out_0, out_1, out_2):
                     )
             return acc
 
-        def finish(i, b, acc):
+        def multiply_by_table(b, acc):
+            products = work.tile([P, 2, GROUP_HEADS, PAIRS, 2], F32, tag="products")
+            shape = [P, GROUP_HEADS, PAIRS, 2, 2]
+            nc.vector.tensor_tensor(
+                out=products[:].rearrange("s w h n e -> s h n w e"),
+                in0=acc[:].rearrange("s (h n w) -> s h n w", h=GROUP_HEADS, w=2).unsqueeze(4).to_broadcast(shape),
+                in1=rot[:, b].unsqueeze(1).to_broadcast(shape),
+                op=ALU.mult,
+            )
+            return products
+
+        def store(i, b, result):
             which, quarter = groups[i]
-            result = results.tile([P, GROUP_HEADS, PAIRS, 2], F32, tag="result")
-            if which == 2:
-                nc.scalar.copy(out=result[:].rearrange("s h n e -> s (h n e)"), in_=acc[:])
-            else:
-                shape = [P, GROUP_HEADS, PAIRS, 2, 2]
-                products = work.tile(shape, F32, tag="products")
-                nc.vector.tensor_tensor(
-                    out=products[:],
-                    in0=acc[:].rearrange("s (h n w) -> s h n w", h=GROUP_HEADS, w=2).unsqueeze(4).to_broadcast(shape),
-                    in1=rot[:, b].unsqueeze(1).to_broadcast(shape),
-                    op=ALU.mult,
-                )
-                nc.vector.tensor_tensor(
-                    out=result[:], in0=products[:, :, :, 0, :], in1=products[:, :, :, 1, :], op=ALU.add
-                )
             first_head = quarter * GROUP_HEADS
             nc.sync.dma_start(
                 out=outputs[which][b, first_head : first_head + GROUP_HEADS].rearrange("h s d -> s h d"),
-                in_=result[:].rearrange("s h n e -> s h (n e)"),
+                in_=result[:].rearrange("s (h d) -> s h d", h=GROUP_HEADS),
             )
 
         def new_operand():
@@ -216,13 +212,26 @@ def tile_ropeattention_pa_kernel(tc, x, coords, W_qkv, out_0, out_1, out_2):
         nc.scalar.activation(out=rot[:], in_=angle[:], func=ACT.Sin)
 
         for i in range(len(groups)):
+            rotated = groups[i][0] != 2
             last = i + 1 == len(groups)
             following = None if last else new_operand()
             for half in range(2):
-                flipped_w = None if last else flip_half(i + 1, half)
-                accs = [multiply(b, ready[0], ready[1]) for b in (2 * half, 2 * half + 1)]
-                finish(i, 2 * half, accs[0])
                 if not last:
-                    quantise_half(half, flipped_w, following[0], following[1])
-                finish(i, 2 * half + 1, accs[1])
+                    quantise_half(half, flip_half(i + 1, half), following[0], following[1])
+                batches = (2 * half, 2 * half + 1)
+                accs = [multiply(b, ready[0], ready[1]) for b in batches]
+                if rotated:
+                    products = [multiply_by_table(b, acc) for b, acc in zip(batches, accs)]
+                for j, b in enumerate(batches):
+                    result = results.tile([P, GROUP_COLS], F32, tag="result")
+                    if rotated:
+                        nc.vector.tensor_tensor(
+                            out=result[:],
+                            in0=products[j][:, 0].rearrange("s h n e -> s (h n e)"),
+                            in1=products[j][:, 1].rearrange("s h n e -> s (h n e)"),
+                            op=ALU.add,
+                        )
+                    else:
+                        nc.scalar.copy(out=result[:], in_=accs[j][:])
+                    store(i, b, result)
             ready = following

@@ -109,7 +109,7 @@ def tile_ropeattention_pa_kernel(tc, x, coords, W_qkv, out_0, out_1, out_2):
         weights = ctx.enter_context(tc.tile_pool(name="weights", bufs=9))
         stage = ctx.enter_context(tc.tile_pool(name="stage", bufs=6))
         packed = ctx.enter_context(tc.tile_pool(name="packed", bufs=3))
-        work = ctx.enter_context(tc.tile_pool(name="work", bufs=4))
+        work = ctx.enter_context(tc.tile_pool(name="work", bufs=6))
         results = ctx.enter_context(tc.tile_pool(name="results", bufs=40))
         flip_psum = ctx.enter_context(tc.psum_pool(name="flip_psum", bufs=4))
         acc_psum = ctx.enter_context(tc.psum_pool(name="acc_psum", bufs=4))
@@ -225,7 +225,7 @@ def tile_ropeattention_pa_kernel(tc, x, coords, W_qkv, out_0, out_1, out_2):
                 for j, b in enumerate(batches):
                     result = results.tile([P, GROUP_COLS], F32, tag="result")
                     if rotated:
-                        nc.vector.tensor_tensor(
+                        nc.gpsimd.tensor_tensor(
                             out=result[:],
                             in0=products[j][:, 0].rearrange("s h n e -> s (h n e)"),
                             in1=products[j][:, 1].rearrange("s h n e -> s (h n e)"),

@@ -14,6 +14,8 @@ ACT = mybir.ActivationFunctionType
 
 P = 128
 BATCH = 4
+PHASES = 4
+RUNS = P // PHASES
 FEATURES = 1536
 HEADS = 16
 HEAD_DIM = 96
@@ -39,23 +41,23 @@ PI_BELOW = 3.1415925
 
 
 def rotation_arguments(nc, const, coords_sb):
-    theta = const.tile([P, BATCH, PAIRS], F32)
-    theta_by_freq = theta[:].rearrange("s b (a j) -> s (b a) j", j=FREQS)
+    theta = const.tile([P, PHASES, PAIRS], F32)
+    theta_by_freq = theta[:].rearrange("p r (a j) -> p (r a) j", j=FREQS)
     for j in range(FREQS):
         nc.vector.tensor_scalar(
             out=theta_by_freq[:, :, j],
-            in0=coords_sb[:].rearrange("s b a -> s (b a)"),
+            in0=coords_sb[:].rearrange("p r a -> p (r a)"),
             scalar1=10000.0 ** (-j / FREQS),
             scalar2=None,
             op0=ALU.mult,
         )
 
-    turns = const.tile([P, BATCH, PAIRS], F32)
+    turns = const.tile([P, PHASES, PAIRS], F32)
     nc.vector.tensor_scalar(
         out=turns[:], in0=theta[:], scalar1=0.5 / math.pi, scalar2=ROUND_MAGIC, op0=ALU.mult, op1=ALU.add
     )
     nc.vector.tensor_scalar(out=turns[:], in0=turns[:], scalar1=ROUND_MAGIC, scalar2=None, op0=ALU.subtract)
-    reduced = const.tile([P, BATCH, PAIRS], F32)
+    reduced = const.tile([P, PHASES, PAIRS], F32)
     nc.vector.scalar_tensor_tensor(
         out=reduced[:], in0=turns[:], scalar=-TURN_HI, in1=theta[:], op0=ALU.mult, op1=ALU.add
     )
@@ -66,12 +68,12 @@ def rotation_arguments(nc, const, coords_sb):
     nc.vector.tensor_scalar(
         out=reduced[:], in0=reduced[:], scalar1=-PI_BELOW, scalar2=PI_BELOW, op0=ALU.max, op1=ALU.min
     )
-    magnitude = const.tile([P, BATCH, PAIRS], F32)
+    magnitude = const.tile([P, PHASES, PAIRS], F32)
     nc.vector.scalar_tensor_tensor(
         out=magnitude[:], in0=reduced[:], scalar=-1.0, in1=reduced[:], op0=ALU.mult, op1=ALU.max
     )
 
-    angle = const.tile([P, BATCH, PAIRS, 2, 2], F32)
+    angle = const.tile([P, PHASES, PAIRS, 2, 2], F32)
     for i in range(2):
         nc.vector.tensor_scalar(
             out=angle[:, :, :, i, i], in0=magnitude[:], scalar1=-1.0, scalar2=0.5 * math.pi,
@@ -82,19 +84,13 @@ def rotation_arguments(nc, const, coords_sb):
     return angle
 
 
-def flip_rows(nc, flip_psum, stage, identity, row_tiles, g):
-    cols = P * len(row_tiles)
-    flipped = flip_psum.tile([P, 2, cols], F32, tag="flipped")
+def flip_rows(nc, flip_psum, selector, row_tiles, g):
+    flipped = flip_psum.tile([P, 2, P * len(row_tiles)], F32, tag="flipped")
     for u in range(2):
         first = PASS_WORDS * g + P * u
         for t, rows in enumerate(row_tiles):
-            nc.tensor.transpose(flipped[:, u, P * t : P * t + P], rows[:, first : first + P], identity[:])
-    grouped = stage.tile([P, 4 * cols], BF16, tag="grouped", align_bytes=64)
-    nc.scalar.copy(
-        out=grouped[:].bitcast(F32).rearrange("q (c u) -> q c u", u=2),
-        in_=flipped[:].rearrange("q u c -> q c u"),
-    )
-    return grouped
+            nc.tensor.transpose(flipped[:, u, P * t : P * t + P], rows[:, first : first + P], selector[:])
+    return flipped
 
 
 def tile_ropeattention_pa_kernel(tc, x, coords, W_qkv, out_0, out_1, out_2):
@@ -106,17 +102,20 @@ def tile_ropeattention_pa_kernel(tc, x, coords, W_qkv, out_0, out_1, out_2):
 
     with ExitStack() as ctx:
         const = ctx.enter_context(tc.tile_pool(name="const", bufs=1))
-        weights = ctx.enter_context(tc.tile_pool(name="weights", bufs=9))
+        weights = ctx.enter_context(tc.tile_pool(name="weights", bufs=8))
         stage = ctx.enter_context(tc.tile_pool(name="stage", bufs=6))
         packed = ctx.enter_context(tc.tile_pool(name="packed", bufs=3))
-        work = ctx.enter_context(tc.tile_pool(name="work", bufs=6))
-        results = ctx.enter_context(tc.tile_pool(name="results", bufs=40))
+        work = ctx.enter_context(tc.tile_pool(name="work", bufs=4))
+        results = ctx.enter_context(tc.tile_pool(name="results", bufs=8))
         flip_psum = ctx.enter_context(tc.psum_pool(name="flip_psum", bufs=4))
         acc_psum = ctx.enter_context(tc.psum_pool(name="acc_psum", bufs=4))
         ctx.enter_context(tc.manual_schedule())
 
-        coords_sb = const.tile([P, BATCH, 3], BF16)
-        nc.scalar.dma_start(out=coords_sb[:], in_=coords.rearrange("b s a -> s b a"))
+        coords_sb = const.tile([P, PHASES, 3], BF16)
+        for b in range(BATCH):
+            nc.scalar.dma_start(
+                out=coords_sb[b:P:BATCH], in_=coords[b].rearrange("(m r) a -> m r a", r=PHASES)
+            )
         x_raw = const.tile([P, BATCH, FEATURES], BF16)
         for b in range(BATCH):
             nc.sync.dma_start(out=x_raw[:, b, :], in_=x[b])
@@ -136,29 +135,41 @@ def tile_ropeattention_pa_kernel(tc, x, coords, W_qkv, out_0, out_1, out_2):
 
         identity = const.tile([P, P], F32)
         make_identity(nc, identity[:])
+        by_phase = const.tile([P, P], F32)
+        nc.vector.tensor_copy(
+            out=by_phase[:].rearrange("s (r m) -> s r m", r=PHASES),
+            in_=identity[:].rearrange("s (m r) -> s r m", r=PHASES),
+        )
         angle = rotation_arguments(nc, const, coords_sb)
 
+        x_words = x_raw[:].bitcast(F32)
+        x_grouped = const.tile([P, PASSES, 4 * BATCH * P], BF16, align_bytes=64)
+        for b in range(0, BATCH, 2):
+            for g in range(PASSES):
+                flipped = flip_rows(nc, flip_psum, by_phase, [x_words[:, b, :], x_words[:, b + 1, :]], g)
+                nc.scalar.copy(
+                    out=x_grouped[:, g, :].bitcast(F32).rearrange("q (c b u) -> q c b u", b=BATCH, u=2)[:, :, b : b + 2, :],
+                    in_=flipped[:].rearrange("q u (b c) -> q c b u", b=2),
+                )
         x_codes = const.tile([P, PASSES, BATCH * P], U32, align_bytes=64)
         x_scales = const.tile([P, PASSES, BATCH * P], U8, align_bytes=64)
-        x_words = x_raw[:].bitcast(F32)
-        for b in range(0, BATCH, 2):
-            flipped_x = [
-                flip_rows(nc, flip_psum, stage, identity, [x_words[:, b, :], x_words[:, b + 1, :]], g)
-                for g in range(PASSES)
-            ]
-            for g in range(PASSES):
-                nc.vector.quantize_mx(
-                    out=x_codes[:, g, P * b : P * b + 2 * P].bitcast(FP8X4),
-                    scales=x_scales[:, g, P * b : P * b + 2 * P],
-                    in_=flipped_x[g][:],
-                )
+        for g in range(PASSES):
+            nc.vector.quantize_mx(
+                out=x_codes[:, g, :].bitcast(FP8X4), scales=x_scales[:, g, :], in_=x_grouped[:, g, :]
+            )
 
         def flip_half(i, half):
             w_words = w_raw[i][:].bitcast(F32)
-            return [
-                flip_rows(nc, flip_psum, stage, identity, [w_words[:, t, :] for t in range(lo // P, hi // P)], g)
-                for g, lo, hi in halves[half]
-            ]
+            flipped_w = []
+            for g, lo, hi in halves[half]:
+                flipped = flip_rows(nc, flip_psum, identity, [w_words[:, t, :] for t in range(lo // P, hi // P)], g)
+                grouped = stage.tile([P, 4 * (hi - lo)], BF16, tag="grouped", align_bytes=64)
+                nc.scalar.copy(
+                    out=grouped[:].bitcast(F32).rearrange("q (c u) -> q c u", u=2),
+                    in_=flipped[:].rearrange("q u c -> q c u"),
+                )
+                flipped_w.append(grouped)
+            return flipped_w
 
         def quantise_half(half, flipped_w, w_codes, w_scales):
             for (g, lo, hi), grouped in zip(halves[half], flipped_w):
@@ -166,14 +177,14 @@ def tile_ropeattention_pa_kernel(tc, x, coords, W_qkv, out_0, out_1, out_2):
                     out=w_codes[:, g, lo:hi].bitcast(FP8X4), scales=w_scales[:, g, lo:hi], in_=grouped[:]
                 )
 
-        def multiply(b, w_codes, w_scales):
+        def multiply(r, w_codes, w_scales):
             acc = acc_psum.tile([P, GROUP_COLS], F32, tag="acc")
             for lo, hi in PARTS:
                 for g in range(PASSES):
                     nc.tensor.matmul_mx(
                         out=acc[:, lo:hi],
-                        lhsT=x_codes[:, g, P * b : P * b + P].bitcast(FP8X4),
-                        lhsT_scale=x_scales[:, g, P * b : P * b + P],
+                        lhsT=x_codes[:, g, P * r : P * r + P].bitcast(FP8X4),
+                        lhsT_scale=x_scales[:, g, P * r : P * r + P],
                         rhs=w_codes[:, g, lo:hi].bitcast(FP8X4),
                         rhs_scale=w_scales[:, g, lo:hi],
                         start=(g == 0),
@@ -181,24 +192,16 @@ def tile_ropeattention_pa_kernel(tc, x, coords, W_qkv, out_0, out_1, out_2):
                     )
             return acc
 
-        def multiply_by_table(b, acc):
+        def multiply_by_table(r, acc):
             products = work.tile([P, 2, GROUP_HEADS, PAIRS, 2], F32, tag="products")
             shape = [P, GROUP_HEADS, PAIRS, 2, 2]
             nc.vector.tensor_tensor(
-                out=products[:].rearrange("s w h n e -> s h n w e"),
-                in0=acc[:].rearrange("s (h n w) -> s h n w", h=GROUP_HEADS, w=2).unsqueeze(4).to_broadcast(shape),
-                in1=rot[:, b].unsqueeze(1).to_broadcast(shape),
+                out=products[:].rearrange("p w h n e -> p h n w e"),
+                in0=acc[:].rearrange("p (h n w) -> p h n w", h=GROUP_HEADS, w=2).unsqueeze(4).to_broadcast(shape),
+                in1=rot[:, r].unsqueeze(1).to_broadcast(shape),
                 op=ALU.mult,
             )
             return products
-
-        def store(i, b, result):
-            which, quarter = groups[i]
-            first_head = quarter * GROUP_HEADS
-            nc.sync.dma_start(
-                out=outputs[which][b, first_head : first_head + GROUP_HEADS].rearrange("h s d -> s h d"),
-                in_=result[:].rearrange("s (h d) -> s h d", h=GROUP_HEADS),
-            )
 
         def new_operand():
             w_codes = packed.tile([P, PASSES, GROUP_COLS], U32, tag="w_codes", align_bytes=64)
@@ -208,30 +211,39 @@ def tile_ropeattention_pa_kernel(tc, x, coords, W_qkv, out_0, out_1, out_2):
         ready = new_operand()
         for half in range(2):
             quantise_half(half, flip_half(0, half), ready[0], ready[1])
-        rot = const.tile([P, BATCH, PAIRS, 2, 2], F32)
+        rot = const.tile([P, PHASES, PAIRS, 2, 2], F32)
         nc.scalar.activation(out=rot[:], in_=angle[:], func=ACT.Sin)
 
         for i in range(len(groups)):
-            rotated = groups[i][0] != 2
+            which, quarter = groups[i]
             last = i + 1 == len(groups)
             following = None if last else new_operand()
+            result = results.tile([P, GROUP_HEADS, PHASES, HEAD_DIM], F32, tag="result")
             for half in range(2):
                 if not last:
                     quantise_half(half, flip_half(i + 1, half), following[0], following[1])
-                batches = (2 * half, 2 * half + 1)
-                accs = [multiply(b, ready[0], ready[1]) for b in batches]
-                if rotated:
-                    products = [multiply_by_table(b, acc) for b, acc in zip(batches, accs)]
-                for j, b in enumerate(batches):
-                    result = results.tile([P, GROUP_COLS], F32, tag="result")
-                    if rotated:
+                phases = (2 * half, 2 * half + 1)
+                accs = [multiply(r, ready[0], ready[1]) for r in phases]
+                if which == 2:
+                    for r, acc in zip(phases, accs):
+                        nc.scalar.copy(
+                            out=result[:, :, r, :], in_=acc[:].rearrange("p (h d) -> p h d", h=GROUP_HEADS)
+                        )
+                else:
+                    products = [multiply_by_table(r, acc) for r, acc in zip(phases, accs)]
+                    for r, planes in zip(phases, products):
                         nc.gpsimd.tensor_tensor(
-                            out=result[:],
-                            in0=products[j][:, 0].rearrange("s h n e -> s (h n e)"),
-                            in1=products[j][:, 1].rearrange("s h n e -> s (h n e)"),
+                            out=result[:, :, r, :],
+                            in0=planes[:, 0].rearrange("p h n e -> p h (n e)"),
+                            in1=planes[:, 1].rearrange("p h n e -> p h (n e)"),
                             op=ALU.add,
                         )
-                    else:
-                        nc.scalar.copy(out=result[:], in_=accs[j][:])
-                    store(i, b, result)
+            first_head = quarter * GROUP_HEADS
+            for b in range(BATCH):
+                nc.sync.dma_start(
+                    out=outputs[which][b, first_head : first_head + GROUP_HEADS].rearrange(
+                        "h (m r) d -> m h (r d)", r=PHASES
+                    ),
+                    in_=result[b:P:BATCH].rearrange("m h r d -> m h (r d)"),
+                )
             ready = following

@@ -14,8 +14,6 @@ ACT = mybir.ActivationFunctionType
 
 P = 128
 BATCH = 4
-PHASES = 4
-RUNS = P // PHASES
 FEATURES = 1536
 HEADS = 16
 HEAD_DIM = 96
@@ -30,6 +28,7 @@ GROUP_COLS = GROUP_HEADS * HEAD_DIM
 GROUP_TILES = GROUP_COLS // P
 GROUPS_PER_OUTPUT = HEADS // GROUP_HEADS
 PARTS = ((0, 2 * P), (2 * P, GROUP_COLS))
+LEAD = 3
 
 FLOPS = 2 * BATCH * P * FEATURES * 3 * HEADS * HEAD_DIM
 
@@ -41,23 +40,23 @@ PI_BELOW = 3.1415925
 
 
 def rotation_arguments(nc, const, coords_sb):
-    theta = const.tile([P, PHASES, PAIRS], F32)
-    theta_by_freq = theta[:].rearrange("p r (a j) -> p (r a) j", j=FREQS)
+    theta = const.tile([P, BATCH, PAIRS], F32)
+    theta_by_freq = theta[:].rearrange("s b (a j) -> s (b a) j", j=FREQS)
     for j in range(FREQS):
         nc.vector.tensor_scalar(
             out=theta_by_freq[:, :, j],
-            in0=coords_sb[:].rearrange("p r a -> p (r a)"),
+            in0=coords_sb[:].rearrange("s b a -> s (b a)"),
             scalar1=10000.0 ** (-j / FREQS),
             scalar2=None,
             op0=ALU.mult,
         )
 
-    turns = const.tile([P, PHASES, PAIRS], F32)
+    turns = const.tile([P, BATCH, PAIRS], F32)
     nc.vector.tensor_scalar(
         out=turns[:], in0=theta[:], scalar1=0.5 / math.pi, scalar2=ROUND_MAGIC, op0=ALU.mult, op1=ALU.add
     )
     nc.vector.tensor_scalar(out=turns[:], in0=turns[:], scalar1=ROUND_MAGIC, scalar2=None, op0=ALU.subtract)
-    reduced = const.tile([P, PHASES, PAIRS], F32)
+    reduced = const.tile([P, BATCH, PAIRS], F32)
     nc.vector.scalar_tensor_tensor(
         out=reduced[:], in0=turns[:], scalar=-TURN_HI, in1=theta[:], op0=ALU.mult, op1=ALU.add
     )
@@ -68,12 +67,12 @@ def rotation_arguments(nc, const, coords_sb):
     nc.vector.tensor_scalar(
         out=reduced[:], in0=reduced[:], scalar1=-PI_BELOW, scalar2=PI_BELOW, op0=ALU.max, op1=ALU.min
     )
-    magnitude = const.tile([P, PHASES, PAIRS], F32)
+    magnitude = const.tile([P, BATCH, PAIRS], F32)
     nc.vector.scalar_tensor_tensor(
         out=magnitude[:], in0=reduced[:], scalar=-1.0, in1=reduced[:], op0=ALU.mult, op1=ALU.max
     )
 
-    angle = const.tile([P, PHASES, PAIRS, 2, 2], F32)
+    angle = const.tile([P, BATCH, PAIRS, 2, 2], F32)
     for i in range(2):
         nc.vector.tensor_scalar(
             out=angle[:, :, :, i, i], in0=magnitude[:], scalar1=-1.0, scalar2=0.5 * math.pi,
@@ -84,42 +83,51 @@ def rotation_arguments(nc, const, coords_sb):
     return angle
 
 
-def flip_rows(nc, flip_psum, selector, row_tiles, g):
-    flipped = flip_psum.tile([P, 2, P * len(row_tiles)], F32, tag="flipped")
+def flip_rows(nc, flip_psum, stage, identity, row_tiles, g):
+    cols = P * len(row_tiles)
+    flipped = flip_psum.tile([P, 2, cols], F32, tag="flipped")
     for u in range(2):
         first = PASS_WORDS * g + P * u
         for t, rows in enumerate(row_tiles):
-            nc.tensor.transpose(flipped[:, u, P * t : P * t + P], rows[:, first : first + P], selector[:])
-    return flipped
+            nc.tensor.transpose(flipped[:, u, P * t : P * t + P], rows[:, first : first + P], identity[:])
+    grouped = stage.tile([P, 4 * cols], BF16, tag="grouped", align_bytes=64)
+    nc.scalar.copy(
+        out=grouped[:].bitcast(F32).rearrange("q (c u) -> q c u", u=2),
+        in_=flipped[:].rearrange("q u c -> q c u"),
+    )
+    return grouped
 
 
 def tile_ropeattention_pa_kernel(tc, x, coords, W_qkv, out_0, out_1, out_2):
     nc = tc.nc
     outputs = (out_0, out_1, out_2)
-    groups = [(which, quarter) for quarter in range(GROUPS_PER_OUTPUT) for which in range(3)]
+    groups = [(which, quarter) for quarter in range(GROUPS_PER_OUTPUT) for which in (0, 2, 1)]
+    units = []
+    for quarter in range(GROUPS_PER_OUTPUT):
+        rotated = [((which, quarter), b) for which in (0, 1) for b in range(BATCH)]
+        for b in range(BATCH):
+            units.extend([rotated[2 * b], rotated[2 * b + 1], ((2, quarter), b)])
     pieces = [(g, lo, hi) for g in range(PASSES) for lo, hi in PARTS]
     halves = (pieces[:3], pieces[3:])
+    half_groups = [(group, half) for group in groups for half in range(2)]
 
     with ExitStack() as ctx:
         const = ctx.enter_context(tc.tile_pool(name="const", bufs=1))
-        weights = ctx.enter_context(tc.tile_pool(name="weights", bufs=8))
+        weights = ctx.enter_context(tc.tile_pool(name="weights", bufs=9))
         stage = ctx.enter_context(tc.tile_pool(name="stage", bufs=6))
-        packed = ctx.enter_context(tc.tile_pool(name="packed", bufs=3))
-        work = ctx.enter_context(tc.tile_pool(name="work", bufs=4))
-        results = ctx.enter_context(tc.tile_pool(name="results", bufs=8))
+        packed = ctx.enter_context(tc.tile_pool(name="packed", bufs=4))
+        work = ctx.enter_context(tc.tile_pool(name="work", bufs=6))
+        results = ctx.enter_context(tc.tile_pool(name="results", bufs=40))
         flip_psum = ctx.enter_context(tc.psum_pool(name="flip_psum", bufs=4))
         acc_psum = ctx.enter_context(tc.psum_pool(name="acc_psum", bufs=4))
         ctx.enter_context(tc.manual_schedule())
 
-        coords_sb = const.tile([P, PHASES, 3], BF16)
-        for b in range(BATCH):
-            nc.scalar.dma_start(
-                out=coords_sb[b:P:BATCH], in_=coords[b].rearrange("(m r) a -> m r a", r=PHASES)
-            )
+        coords_sb = const.tile([P, BATCH, 3], BF16)
+        nc.scalar.dma_start(out=coords_sb[:], in_=coords.rearrange("b s a -> s b a"))
         x_raw = const.tile([P, BATCH, FEATURES], BF16)
         for b in range(BATCH):
             nc.sync.dma_start(out=x_raw[:, b, :], in_=x[b])
-        w_raw = []
+        w_raw = {}
         for which, quarter in groups:
             first_row = which * HEADS * HEAD_DIM + quarter * GROUP_COLS
             w_rows = weights.tile([P, GROUP_TILES, FEATURES], BF16, tag="w_rows")
@@ -127,7 +135,7 @@ def tile_ropeattention_pa_kernel(tc, x, coords, W_qkv, out_0, out_1, out_2):
                 out=w_rows[:],
                 in_=W_qkv[first_row : first_row + GROUP_COLS, :].rearrange("(t p) k -> p t k", p=P),
             )
-            w_raw.append(w_rows)
+            w_raw[(which, quarter)] = w_rows
 
         warm = const.tile([P, 1], F32)
         nc.vector.memset(warm[:], 0.0)
@@ -135,41 +143,29 @@ def tile_ropeattention_pa_kernel(tc, x, coords, W_qkv, out_0, out_1, out_2):
 
         identity = const.tile([P, P], F32)
         make_identity(nc, identity[:])
-        by_phase = const.tile([P, P], F32)
-        nc.vector.tensor_copy(
-            out=by_phase[:].rearrange("s (r m) -> s r m", r=PHASES),
-            in_=identity[:].rearrange("s (m r) -> s r m", r=PHASES),
-        )
         angle = rotation_arguments(nc, const, coords_sb)
 
-        x_words = x_raw[:].bitcast(F32)
-        x_grouped = const.tile([P, PASSES, 4 * BATCH * P], BF16, align_bytes=64)
-        for b in range(0, BATCH, 2):
-            for g in range(PASSES):
-                flipped = flip_rows(nc, flip_psum, by_phase, [x_words[:, b, :], x_words[:, b + 1, :]], g)
-                nc.scalar.copy(
-                    out=x_grouped[:, g, :].bitcast(F32).rearrange("q (c b u) -> q c b u", b=BATCH, u=2)[:, :, b : b + 2, :],
-                    in_=flipped[:].rearrange("q u (b c) -> q c b u", b=2),
-                )
         x_codes = const.tile([P, PASSES, BATCH * P], U32, align_bytes=64)
         x_scales = const.tile([P, PASSES, BATCH * P], U8, align_bytes=64)
-        for g in range(PASSES):
-            nc.vector.quantize_mx(
-                out=x_codes[:, g, :].bitcast(FP8X4), scales=x_scales[:, g, :], in_=x_grouped[:, g, :]
-            )
-
-        def flip_half(i, half):
-            w_words = w_raw[i][:].bitcast(F32)
-            flipped_w = []
-            for g, lo, hi in halves[half]:
-                flipped = flip_rows(nc, flip_psum, identity, [w_words[:, t, :] for t in range(lo // P, hi // P)], g)
-                grouped = stage.tile([P, 4 * (hi - lo)], BF16, tag="grouped", align_bytes=64)
-                nc.scalar.copy(
-                    out=grouped[:].bitcast(F32).rearrange("q (c u) -> q c u", u=2),
-                    in_=flipped[:].rearrange("q u c -> q c u"),
+        x_words = x_raw[:].bitcast(F32)
+        for b in range(0, BATCH, 2):
+            flipped_x = [
+                flip_rows(nc, flip_psum, stage, identity, [x_words[:, b, :], x_words[:, b + 1, :]], g)
+                for g in range(PASSES)
+            ]
+            for g in range(PASSES):
+                nc.vector.quantize_mx(
+                    out=x_codes[:, g, P * b : P * b + 2 * P].bitcast(FP8X4),
+                    scales=x_scales[:, g, P * b : P * b + 2 * P],
+                    in_=flipped_x[g][:],
                 )
-                flipped_w.append(grouped)
-            return flipped_w
+
+        def flip_half(group, half):
+            w_words = w_raw[group][:].bitcast(F32)
+            return [
+                flip_rows(nc, flip_psum, stage, identity, [w_words[:, t, :] for t in range(lo // P, hi // P)], g)
+                for g, lo, hi in halves[half]
+            ]
 
         def quantise_half(half, flipped_w, w_codes, w_scales):
             for (g, lo, hi), grouped in zip(halves[half], flipped_w):
@@ -177,14 +173,14 @@ def tile_ropeattention_pa_kernel(tc, x, coords, W_qkv, out_0, out_1, out_2):
                     out=w_codes[:, g, lo:hi].bitcast(FP8X4), scales=w_scales[:, g, lo:hi], in_=grouped[:]
                 )
 
-        def multiply(r, w_codes, w_scales):
+        def multiply(b, w_codes, w_scales):
             acc = acc_psum.tile([P, GROUP_COLS], F32, tag="acc")
             for lo, hi in PARTS:
                 for g in range(PASSES):
                     nc.tensor.matmul_mx(
                         out=acc[:, lo:hi],
-                        lhsT=x_codes[:, g, P * r : P * r + P].bitcast(FP8X4),
-                        lhsT_scale=x_scales[:, g, P * r : P * r + P],
+                        lhsT=x_codes[:, g, P * b : P * b + P].bitcast(FP8X4),
+                        lhsT_scale=x_scales[:, g, P * b : P * b + P],
                         rhs=w_codes[:, g, lo:hi].bitcast(FP8X4),
                         rhs_scale=w_scales[:, g, lo:hi],
                         start=(g == 0),
@@ -192,58 +188,56 @@ def tile_ropeattention_pa_kernel(tc, x, coords, W_qkv, out_0, out_1, out_2):
                     )
             return acc
 
-        def multiply_by_table(r, acc):
+        def multiply_by_table(b, acc):
             products = work.tile([P, 2, GROUP_HEADS, PAIRS, 2], F32, tag="products")
             shape = [P, GROUP_HEADS, PAIRS, 2, 2]
             nc.vector.tensor_tensor(
-                out=products[:].rearrange("p w h n e -> p h n w e"),
-                in0=acc[:].rearrange("p (h n w) -> p h n w", h=GROUP_HEADS, w=2).unsqueeze(4).to_broadcast(shape),
-                in1=rot[:, r].unsqueeze(1).to_broadcast(shape),
+                out=products[:].rearrange("s w h n e -> s h n w e"),
+                in0=acc[:].rearrange("s (h n w) -> s h n w", h=GROUP_HEADS, w=2).unsqueeze(4).to_broadcast(shape),
+                in1=rot[:, b].unsqueeze(1).to_broadcast(shape),
                 op=ALU.mult,
             )
             return products
 
-        def new_operand():
-            w_codes = packed.tile([P, PASSES, GROUP_COLS], U32, tag="w_codes", align_bytes=64)
-            w_scales = packed.tile([P, PASSES, GROUP_COLS], U8, tag="w_scales", align_bytes=64)
-            return w_codes, w_scales
+        def store(group, b, result):
+            which, quarter = group
+            first_head = quarter * GROUP_HEADS
+            nc.sync.dma_start(
+                out=outputs[which][b, first_head : first_head + GROUP_HEADS].rearrange("h s d -> s h d"),
+                in_=result[:].rearrange("s (h d) -> s h d", h=GROUP_HEADS),
+            )
 
-        ready = new_operand()
-        for half in range(2):
-            quantise_half(half, flip_half(0, half), ready[0], ready[1])
-        rot = const.tile([P, PHASES, PAIRS, 2, 2], F32)
+        operands = {}
+
+        def prepare(group, half):
+            if half == 0:
+                w_codes = packed.tile([P, PASSES, GROUP_COLS], U32, tag="w_codes", align_bytes=64)
+                w_scales = packed.tile([P, PASSES, GROUP_COLS], U8, tag="w_scales", align_bytes=64)
+                operands[group] = (w_codes, w_scales)
+            quantise_half(half, flip_half(group, half), *operands[group])
+
+        for group, half in half_groups[:LEAD]:
+            prepare(group, half)
+        rot = const.tile([P, BATCH, PAIRS, 2, 2], F32)
         nc.scalar.activation(out=rot[:], in_=angle[:], func=ACT.Sin)
 
-        for i in range(len(groups)):
-            which, quarter = groups[i]
-            last = i + 1 == len(groups)
-            following = None if last else new_operand()
-            result = results.tile([P, GROUP_HEADS, PHASES, HEAD_DIM], F32, tag="result")
-            for half in range(2):
-                if not last:
-                    quantise_half(half, flip_half(i + 1, half), following[0], following[1])
-                phases = (2 * half, 2 * half + 1)
-                accs = [multiply(r, ready[0], ready[1]) for r in phases]
-                if which == 2:
-                    for r, acc in zip(phases, accs):
-                        nc.scalar.copy(
-                            out=result[:, :, r, :], in_=acc[:].rearrange("p (h d) -> p h d", h=GROUP_HEADS)
-                        )
+        for step in range(len(units) // 2):
+            for group, half in half_groups[step + LEAD : step + LEAD + 1]:
+                prepare(group, half)
+            pair = units[2 * step : 2 * step + 2]
+            accs = [multiply(b, *operands[group]) for group, b in pair]
+            products = [
+                multiply_by_table(b, acc) if group[0] != 2 else None for (group, b), acc in zip(pair, accs)
+            ]
+            for (group, b), acc, planes in zip(pair, accs, products):
+                result = results.tile([P, GROUP_COLS], F32, tag="result")
+                if planes is None:
+                    nc.scalar.copy(out=result[:], in_=acc[:])
                 else:
-                    products = [multiply_by_table(r, acc) for r, acc in zip(phases, accs)]
-                    for r, planes in zip(phases, products):
-                        nc.gpsimd.tensor_tensor(
-                            out=result[:, :, r, :],
-                            in0=planes[:, 0].rearrange("p h n e -> p h (n e)"),
-                            in1=planes[:, 1].rearrange("p h n e -> p h (n e)"),
-                            op=ALU.add,
-                        )
-            first_head = quarter * GROUP_HEADS
-            for b in range(BATCH):
-                nc.sync.dma_start(
-                    out=outputs[which][b, first_head : first_head + GROUP_HEADS].rearrange(
-                        "h (m r) d -> m h (r d)", r=PHASES
-                    ),
-                    in_=result[b:P:BATCH].rearrange("m h r d -> m h (r d)"),
-                )
-            ready = following
+                    nc.gpsimd.tensor_tensor(
+                        out=result[:],
+                        in0=planes[:, 0].rearrange("s h n e -> s (h n e)"),
+                        in1=planes[:, 1].rearrange("s h n e -> s (h n e)"),
+                        op=ALU.add,
+                    )
+                store(group, b, result)

@@ -14,6 +14,8 @@ ACT = mybir.ActivationFunctionType
 
 P = 128
 BATCH = 4
+PHASES = 4
+RUNS = P // PHASES
 FEATURES = 1536
 HEADS = 16
 HEAD_DIM = 96
@@ -40,23 +42,23 @@ PI_BELOW = 3.1415925
 
 
 def rotation_arguments(nc, const, coords_sb):
-    theta = const.tile([P, BATCH, PAIRS], F32)
-    theta_by_freq = theta[:].rearrange("s b (a j) -> s (b a) j", j=FREQS)
+    theta = const.tile([P, PHASES, PAIRS], F32)
+    theta_by_freq = theta[:].rearrange("p r (a j) -> p (r a) j", j=FREQS)
     for j in range(FREQS):
         nc.vector.tensor_scalar(
             out=theta_by_freq[:, :, j],
-            in0=coords_sb[:].rearrange("s b a -> s (b a)"),
+            in0=coords_sb[:].rearrange("p r a -> p (r a)"),
             scalar1=10000.0 ** (-j / FREQS),
             scalar2=None,
             op0=ALU.mult,
         )
 
-    turns = const.tile([P, BATCH, PAIRS], F32)
+    turns = const.tile([P, PHASES, PAIRS], F32)
     nc.vector.tensor_scalar(
         out=turns[:], in0=theta[:], scalar1=0.5 / math.pi, scalar2=ROUND_MAGIC, op0=ALU.mult, op1=ALU.add
     )
     nc.vector.tensor_scalar(out=turns[:], in0=turns[:], scalar1=ROUND_MAGIC, scalar2=None, op0=ALU.subtract)
-    reduced = const.tile([P, BATCH, PAIRS], F32)
+    reduced = const.tile([P, PHASES, PAIRS], F32)
     nc.vector.scalar_tensor_tensor(
         out=reduced[:], in0=turns[:], scalar=-TURN_HI, in1=theta[:], op0=ALU.mult, op1=ALU.add
     )
@@ -67,12 +69,12 @@ def rotation_arguments(nc, const, coords_sb):
     nc.vector.tensor_scalar(
         out=reduced[:], in0=reduced[:], scalar1=-PI_BELOW, scalar2=PI_BELOW, op0=ALU.max, op1=ALU.min
     )
-    magnitude = const.tile([P, BATCH, PAIRS], F32)
+    magnitude = const.tile([P, PHASES, PAIRS], F32)
     nc.vector.scalar_tensor_tensor(
         out=magnitude[:], in0=reduced[:], scalar=-1.0, in1=reduced[:], op0=ALU.mult, op1=ALU.max
     )
 
-    angle = const.tile([P, BATCH, PAIRS, 2, 2], F32)
+    angle = const.tile([P, PHASES, PAIRS, 2, 2], F32)
     for i in range(2):
         nc.vector.tensor_scalar(
             out=angle[:, :, :, i, i], in0=magnitude[:], scalar1=-1.0, scalar2=0.5 * math.pi,
@@ -83,19 +85,13 @@ def rotation_arguments(nc, const, coords_sb):
     return angle
 
 
-def flip_rows(nc, flip_psum, stage, identity, row_tiles, g):
-    cols = P * len(row_tiles)
-    flipped = flip_psum.tile([P, 2, cols], F32, tag="flipped")
+def flip_rows(nc, flip_psum, selector, row_tiles, g):
+    flipped = flip_psum.tile([P, 2, P * len(row_tiles)], F32, tag="flipped")
     for u in range(2):
         first = PASS_WORDS * g + P * u
         for t, rows in enumerate(row_tiles):
-            nc.tensor.transpose(flipped[:, u, P * t : P * t + P], rows[:, first : first + P], identity[:])
-    grouped = stage.tile([P, 4 * cols], BF16, tag="grouped", align_bytes=64)
-    nc.scalar.copy(
-        out=grouped[:].bitcast(F32).rearrange("q (c u) -> q c u", u=2),
-        in_=flipped[:].rearrange("q u c -> q c u"),
-    )
-    return grouped
+            nc.tensor.transpose(flipped[:, u, P * t : P * t + P], rows[:, first : first + P], selector[:])
+    return flipped
 
 
 def tile_ropeattention_pa_kernel(tc, x, coords, W_qkv, out_0, out_1, out_2):
@@ -104,26 +100,29 @@ def tile_ropeattention_pa_kernel(tc, x, coords, W_qkv, out_0, out_1, out_2):
     groups = [(which, quarter) for quarter in range(GROUPS_PER_OUTPUT) for which in (0, 2, 1)]
     units = []
     for quarter in range(GROUPS_PER_OUTPUT):
-        rotated = [((which, quarter), b) for which in (0, 1) for b in range(BATCH)]
-        for b in range(BATCH):
-            units.extend([rotated[2 * b], rotated[2 * b + 1], ((2, quarter), b)])
+        rotated = [((which, quarter), r) for which in (0, 1) for r in range(PHASES)]
+        for r in range(PHASES):
+            units.extend([rotated[2 * r], rotated[2 * r + 1], ((2, quarter), r)])
     pieces = [(g, lo, hi) for g in range(PASSES) for lo, hi in PARTS]
     halves = (pieces[:3], pieces[3:])
     half_groups = [(group, half) for group in groups for half in range(2)]
 
     with ExitStack() as ctx:
         const = ctx.enter_context(tc.tile_pool(name="const", bufs=1))
-        weights = ctx.enter_context(tc.tile_pool(name="weights", bufs=9))
+        weights = ctx.enter_context(tc.tile_pool(name="weights", bufs=8))
         stage = ctx.enter_context(tc.tile_pool(name="stage", bufs=6))
         packed = ctx.enter_context(tc.tile_pool(name="packed", bufs=4))
         work = ctx.enter_context(tc.tile_pool(name="work", bufs=6))
-        results = ctx.enter_context(tc.tile_pool(name="results", bufs=40))
+        results = ctx.enter_context(tc.tile_pool(name="results", bufs=8))
         flip_psum = ctx.enter_context(tc.psum_pool(name="flip_psum", bufs=4))
         acc_psum = ctx.enter_context(tc.psum_pool(name="acc_psum", bufs=4))
         ctx.enter_context(tc.manual_schedule())
 
-        coords_sb = const.tile([P, BATCH, 3], BF16)
-        nc.scalar.dma_start(out=coords_sb[:], in_=coords.rearrange("b s a -> s b a"))
+        coords_sb = const.tile([P, PHASES, 3], BF16)
+        for b in range(BATCH):
+            nc.scalar.dma_start(
+                out=coords_sb[b:P:BATCH], in_=coords[b].rearrange("(m r) a -> m r a", r=PHASES)
+            )
         x_raw = const.tile([P, BATCH, FEATURES], BF16)
         for b in range(BATCH):
             nc.sync.dma_start(out=x_raw[:, b, :], in_=x[b])
@@ -143,29 +142,41 @@ def tile_ropeattention_pa_kernel(tc, x, coords, W_qkv, out_0, out_1, out_2):
 
         identity = const.tile([P, P], F32)
         make_identity(nc, identity[:])
+        by_phase = const.tile([P, P], F32)
+        nc.vector.tensor_copy(
+            out=by_phase[:].rearrange("s (r m) -> s r m", r=PHASES),
+            in_=identity[:].rearrange("s (m r) -> s r m", r=PHASES),
+        )
         angle = rotation_arguments(nc, const, coords_sb)
 
+        x_words = x_raw[:].bitcast(F32)
+        x_grouped = const.tile([P, PASSES, 4 * BATCH * P], BF16, align_bytes=64)
+        for b in range(0, BATCH, 2):
+            for g in range(PASSES):
+                flipped = flip_rows(nc, flip_psum, by_phase, [x_words[:, b, :], x_words[:, b + 1, :]], g)
+                nc.scalar.copy(
+                    out=x_grouped[:, g, :].bitcast(F32).rearrange("q (c b u) -> q c b u", b=BATCH, u=2)[:, :, b : b + 2, :],
+                    in_=flipped[:].rearrange("q u (b c) -> q c b u", b=2),
+                )
         x_codes = const.tile([P, PASSES, BATCH * P], U32, align_bytes=64)
         x_scales = const.tile([P, PASSES, BATCH * P], U8, align_bytes=64)
-        x_words = x_raw[:].bitcast(F32)
-        for b in range(0, BATCH, 2):
-            flipped_x = [
-                flip_rows(nc, flip_psum, stage, identity, [x_words[:, b, :], x_words[:, b + 1, :]], g)
-                for g in range(PASSES)
-            ]
-            for g in range(PASSES):
-                nc.vector.quantize_mx(
-                    out=x_codes[:, g, P * b : P * b + 2 * P].bitcast(FP8X4),
-                    scales=x_scales[:, g, P * b : P * b + 2 * P],
-                    in_=flipped_x[g][:],
-                )
+        for g in range(PASSES):
+            nc.vector.quantize_mx(
+                out=x_codes[:, g, :].bitcast(FP8X4), scales=x_scales[:, g, :], in_=x_grouped[:, g, :]
+            )
 
         def flip_half(group, half):
             w_words = w_raw[group][:].bitcast(F32)
-            return [
-                flip_rows(nc, flip_psum, stage, identity, [w_words[:, t, :] for t in range(lo // P, hi // P)], g)
-                for g, lo, hi in halves[half]
-            ]
+            flipped_w = []
+            for g, lo, hi in halves[half]:
+                flipped = flip_rows(nc, flip_psum, identity, [w_words[:, t, :] for t in range(lo // P, hi // P)], g)
+                grouped = stage.tile([P, 4 * (hi - lo)], BF16, tag="grouped", align_bytes=64)
+                nc.scalar.copy(
+                    out=grouped[:].bitcast(F32).rearrange("q (c u) -> q c u", u=2),
+                    in_=flipped[:].rearrange("q u c -> q c u"),
+                )
+                flipped_w.append(grouped)
+            return flipped_w
 
         def quantise_half(half, flipped_w, w_codes, w_scales):
             for (g, lo, hi), grouped in zip(halves[half], flipped_w):
@@ -173,14 +184,14 @@ def tile_ropeattention_pa_kernel(tc, x, coords, W_qkv, out_0, out_1, out_2):
                     out=w_codes[:, g, lo:hi].bitcast(FP8X4), scales=w_scales[:, g, lo:hi], in_=grouped[:]
                 )
 
-        def multiply(b, w_codes, w_scales):
+        def multiply(r, w_codes, w_scales):
             acc = acc_psum.tile([P, GROUP_COLS], F32, tag="acc")
             for lo, hi in PARTS:
                 for g in range(PASSES):
                     nc.tensor.matmul_mx(
                         out=acc[:, lo:hi],
-                        lhsT=x_codes[:, g, P * b : P * b + P].bitcast(FP8X4),
-                        lhsT_scale=x_scales[:, g, P * b : P * b + P],
+                        lhsT=x_codes[:, g, P * r : P * r + P].bitcast(FP8X4),
+                        lhsT_scale=x_scales[:, g, P * r : P * r + P],
                         rhs=w_codes[:, g, lo:hi].bitcast(FP8X4),
                         rhs_scale=w_scales[:, g, lo:hi],
                         start=(g == 0),
@@ -188,26 +199,19 @@ def tile_ropeattention_pa_kernel(tc, x, coords, W_qkv, out_0, out_1, out_2):
                     )
             return acc
 
-        def multiply_by_table(b, acc):
+        def multiply_by_table(r, acc):
             products = work.tile([P, 2, GROUP_HEADS, PAIRS, 2], F32, tag="products")
             shape = [P, GROUP_HEADS, PAIRS, 2, 2]
             nc.vector.tensor_tensor(
-                out=products[:].rearrange("s w h n e -> s h n w e"),
-                in0=acc[:].rearrange("s (h n w) -> s h n w", h=GROUP_HEADS, w=2).unsqueeze(4).to_broadcast(shape),
-                in1=rot[:, b].unsqueeze(1).to_broadcast(shape),
+                out=products[:].rearrange("p w h n e -> p h n w e"),
+                in0=acc[:].rearrange("p (h n w) -> p h n w", h=GROUP_HEADS, w=2).unsqueeze(4).to_broadcast(shape),
+                in1=rot[:, r].unsqueeze(1).to_broadcast(shape),
                 op=ALU.mult,
             )
             return products
 
-        def store(group, b, result):
-            which, quarter = group
-            first_head = quarter * GROUP_HEADS
-            nc.sync.dma_start(
-                out=outputs[which][b, first_head : first_head + GROUP_HEADS].rearrange("h s d -> s h d"),
-                in_=result[:].rearrange("s (h d) -> s h d", h=GROUP_HEADS),
-            )
-
         operands = {}
+        finished = {}
 
         def prepare(group, half):
             if half == 0:
@@ -216,28 +220,44 @@ def tile_ropeattention_pa_kernel(tc, x, coords, W_qkv, out_0, out_1, out_2):
                 operands[group] = (w_codes, w_scales)
             quantise_half(half, flip_half(group, half), *operands[group])
 
+        def store(group):
+            which, quarter = group
+            first_head = quarter * GROUP_HEADS
+            for b in range(BATCH):
+                nc.sync.dma_start(
+                    out=outputs[which][b, first_head : first_head + GROUP_HEADS].rearrange(
+                        "h (m r) d -> m h (r d)", r=PHASES
+                    ),
+                    in_=finished[group][b:P:BATCH].rearrange("m h r d -> m h (r d)"),
+                )
+
         for group, half in half_groups[:LEAD]:
             prepare(group, half)
-        rot = const.tile([P, BATCH, PAIRS, 2, 2], F32)
+        rot = const.tile([P, PHASES, PAIRS, 2, 2], F32)
         nc.scalar.activation(out=rot[:], in_=angle[:], func=ACT.Sin)
 
         for step in range(len(units) // 2):
             for group, half in half_groups[step + LEAD : step + LEAD + 1]:
                 prepare(group, half)
             pair = units[2 * step : 2 * step + 2]
-            accs = [multiply(b, *operands[group]) for group, b in pair]
+            accs = [multiply(r, *operands[group]) for group, r in pair]
             products = [
-                multiply_by_table(b, acc) if group[0] != 2 else None for (group, b), acc in zip(pair, accs)
+                multiply_by_table(r, acc) if group[0] != 2 else None for (group, r), acc in zip(pair, accs)
             ]
-            for (group, b), acc, planes in zip(pair, accs, products):
-                result = results.tile([P, GROUP_COLS], F32, tag="result")
+            for (group, r), acc, planes in zip(pair, accs, products):
+                if r == 0:
+                    result = results.tile([P, GROUP_HEADS, PHASES, HEAD_DIM], F32, tag="result")
+                    finished[group] = result
                 if planes is None:
-                    nc.scalar.copy(out=result[:], in_=acc[:])
+                    nc.scalar.copy(
+                        out=finished[group][:, :, r, :], in_=acc[:].rearrange("p (h d) -> p h d", h=GROUP_HEADS)
+                    )
                 else:
                     nc.gpsimd.tensor_tensor(
-                        out=result[:],
-                        in0=planes[:, 0].rearrange("s h n e -> s (h n e)"),
-                        in1=planes[:, 1].rearrange("s h n e -> s (h n e)"),
+                        out=finished[group][:, :, r, :],
+                        in0=planes[:, 0].rearrange("p h n e -> p h (n e)"),
+                        in1=planes[:, 1].rearrange("p h n e -> p h (n e)"),
                         op=ALU.add,
                     )
-                store(group, b, result)
+                if r == PHASES - 1:
+                    store(group)

import math
from contextlib import ExitStack

import concourse.mybir as mybir
from concourse.masks import make_identity

F32 = mybir.dt.float32
BF16 = mybir.dt.bfloat16
U32 = mybir.dt.uint32
U8 = mybir.dt.uint8
FP8X4 = mybir.dt.float8_e4m3fn_x4
ALU = mybir.AluOpType
ACT = mybir.ActivationFunctionType

P = 128
BATCH = 4
PHASES = 4
RUNS = P // PHASES
FEATURES = 1536
HEADS = 16
HEAD_DIM = 96
PAIRS = HEAD_DIM // 2
FREQS = HEAD_DIM // 6
K_PASS = 512
PASSES = FEATURES // K_PASS
PASS_WORDS = K_PASS // 2

GROUP_HEADS = 4
GROUP_COLS = GROUP_HEADS * HEAD_DIM
GROUP_TILES = GROUP_COLS // P
GROUPS_PER_OUTPUT = HEADS // GROUP_HEADS
PARTS = ((0, 2 * P), (2 * P, GROUP_COLS))
LEAD = 3

FLOPS = 2 * BATCH * P * FEATURES * 3 * HEADS * HEAD_DIM

TURN_HI = 6.28125
TURN_MID = 4059.0 / 2097152.0
TURN_LO = 2.0 * math.pi - TURN_HI - TURN_MID
ROUND_MAGIC = 12582912.0
PI_BELOW = 3.1415925


def rotation_arguments(nc, const, coords_sb):
    theta = const.tile([P, PHASES, PAIRS], F32)
    theta_by_freq = theta[:].rearrange("p r (a j) -> p (r a) j", j=FREQS)
    for j in range(FREQS):
        nc.vector.tensor_scalar(
            out=theta_by_freq[:, :, j],
            in0=coords_sb[:].rearrange("p r a -> p (r a)"),
            scalar1=10000.0 ** (-j / FREQS),
            scalar2=None,
            op0=ALU.mult,
        )

    turns = const.tile([P, PHASES, PAIRS], F32)
    nc.vector.tensor_scalar(
        out=turns[:], in0=theta[:], scalar1=0.5 / math.pi, scalar2=ROUND_MAGIC, op0=ALU.mult, op1=ALU.add
    )
    nc.vector.tensor_scalar(out=turns[:], in0=turns[:], scalar1=ROUND_MAGIC, scalar2=None, op0=ALU.subtract)
    reduced = const.tile([P, PHASES, PAIRS], F32)
    nc.vector.scalar_tensor_tensor(
        out=reduced[:], in0=turns[:], scalar=-TURN_HI, in1=theta[:], op0=ALU.mult, op1=ALU.add
    )
    for piece in (TURN_MID, TURN_LO):
        nc.vector.scalar_tensor_tensor(
            out=reduced[:], in0=turns[:], scalar=-piece, in1=reduced[:], op0=ALU.mult, op1=ALU.add
        )
    nc.vector.tensor_scalar(
        out=reduced[:], in0=reduced[:], scalar1=-PI_BELOW, scalar2=PI_BELOW, op0=ALU.max, op1=ALU.min
    )
    magnitude = const.tile([P, PHASES, PAIRS], F32)
    nc.vector.scalar_tensor_tensor(
        out=magnitude[:], in0=reduced[:], scalar=-1.0, in1=reduced[:], op0=ALU.mult, op1=ALU.max
    )

    angle = const.tile([P, PHASES, PAIRS, 2, 2], F32)
    for i in range(2):
        nc.vector.tensor_scalar(
            out=angle[:, :, :, i, i], in0=magnitude[:], scalar1=-1.0, scalar2=0.5 * math.pi,
            op0=ALU.mult, op1=ALU.add,
        )
    nc.vector.tensor_copy(out=angle[:, :, :, 0, 1], in_=reduced[:])
    nc.vector.tensor_scalar(out=angle[:, :, :, 1, 0], in0=reduced[:], scalar1=-1.0, scalar2=None, op0=ALU.mult)
    return angle


def flip_rows(nc, flip_psum, selector, row_tiles, g):
    flipped = flip_psum.tile([P, 2, P * len(row_tiles)], F32, tag="flipped")
    for u in range(2):
        first = PASS_WORDS * g + P * u
        for t, rows in enumerate(row_tiles):
            nc.tensor.transpose(flipped[:, u, P * t : P * t + P], rows[:, first : first + P], selector[:])
    return flipped


def tile_ropeattention_pa_kernel(tc, x, coords, W_qkv, out_0, out_1, out_2):
    nc = tc.nc
    outputs = (out_0, out_1, out_2)
    groups = [(which, quarter) for quarter in range(GROUPS_PER_OUTPUT) for which in (0, 2, 1)]
    units = []
    for quarter in range(GROUPS_PER_OUTPUT):
        rotated = [((which, quarter), r) for which in (0, 1) for r in range(PHASES)]
        for r in range(PHASES):
            units.extend([rotated[2 * r], rotated[2 * r + 1], ((2, quarter), r)])
    pieces = [(g, lo, hi) for g in range(PASSES) for lo, hi in PARTS]
    halves = (pieces[:3], pieces[3:])
    half_groups = [(group, half) for group in groups for half in range(2)]

    with ExitStack() as ctx:
        const = ctx.enter_context(tc.tile_pool(name="const", bufs=1))
        weights = ctx.enter_context(tc.tile_pool(name="weights", bufs=8))
        stage = ctx.enter_context(tc.tile_pool(name="stage", bufs=6))
        packed = ctx.enter_context(tc.tile_pool(name="packed", bufs=4))
        work = ctx.enter_context(tc.tile_pool(name="work", bufs=6))
        results = ctx.enter_context(tc.tile_pool(name="results", bufs=8))
        flip_psum = ctx.enter_context(tc.psum_pool(name="flip_psum", bufs=4))
        acc_psum = ctx.enter_context(tc.psum_pool(name="acc_psum", bufs=4))
        ctx.enter_context(tc.manual_schedule())

        coords_sb = const.tile([P, PHASES, 3], BF16)
        for b in range(BATCH):
            nc.scalar.dma_start(
                out=coords_sb[b:P:BATCH], in_=coords[b].rearrange("(m r) a -> m r a", r=PHASES)
            )
        x_raw = const.tile([P, BATCH, FEATURES], BF16)
        for b in range(BATCH):
            nc.sync.dma_start(out=x_raw[:, b, :], in_=x[b])
        w_raw = {}
        for which, quarter in groups:
            first_row = which * HEADS * HEAD_DIM + quarter * GROUP_COLS
            w_rows = weights.tile([P, GROUP_TILES, FEATURES], BF16, tag="w_rows")
            nc.sync.dma_start(
                out=w_rows[:],
                in_=W_qkv[first_row : first_row + GROUP_COLS, :].rearrange("(t p) k -> p t k", p=P),
            )
            w_raw[(which, quarter)] = w_rows

        warm = const.tile([P, 1], F32)
        nc.vector.memset(warm[:], 0.0)
        nc.scalar.activation(out=warm[:], in_=warm[:], func=ACT.Sin)

        identity = const.tile([P, P], F32)
        make_identity(nc, identity[:])
        by_phase = const.tile([P, P], F32)
        nc.vector.tensor_copy(
            out=by_phase[:].rearrange("s (r m) -> s r m", r=PHASES),
            in_=identity[:].rearrange("s (m r) -> s r m", r=PHASES),
        )
        angle = rotation_arguments(nc, const, coords_sb)

        x_words = x_raw[:].bitcast(F32)
        x_grouped = const.tile([P, PASSES, 4 * BATCH * P], BF16, align_bytes=64)
        for b in range(0, BATCH, 2):
            for g in range(PASSES):
                flipped = flip_rows(nc, flip_psum, by_phase, [x_words[:, b, :], x_words[:, b + 1, :]], g)
                nc.scalar.copy(
                    out=x_grouped[:, g, :].bitcast(F32).rearrange("q (c b u) -> q c b u", b=BATCH, u=2)[:, :, b : b + 2, :],
                    in_=flipped[:].rearrange("q u (b c) -> q c b u", b=2),
                )
        x_codes = const.tile([P, PASSES, BATCH * P], U32, align_bytes=64)
        x_scales = const.tile([P, PASSES, BATCH * P], U8, align_bytes=64)
        for g in range(PASSES):
            nc.vector.quantize_mx(
                out=x_codes[:, g, :].bitcast(FP8X4), scales=x_scales[:, g, :], in_=x_grouped[:, g, :]
            )

        def flip_half(group, half):
            w_words = w_raw[group][:].bitcast(F32)
            flipped_w = []
            for g, lo, hi in halves[half]:
                flipped = flip_rows(nc, flip_psum, identity, [w_words[:, t, :] for t in range(lo // P, hi // P)], g)
                grouped = stage.tile([P, 4 * (hi - lo)], BF16, tag="grouped", align_bytes=64)
                nc.scalar.copy(
                    out=grouped[:].bitcast(F32).rearrange("q (c u) -> q c u", u=2),
                    in_=flipped[:].rearrange("q u c -> q c u"),
                )
                flipped_w.append(grouped)
            return flipped_w

        def quantise_half(half, flipped_w, w_codes, w_scales):
            for (g, lo, hi), grouped in zip(halves[half], flipped_w):
                nc.vector.quantize_mx(
                    out=w_codes[:, g, lo:hi].bitcast(FP8X4), scales=w_scales[:, g, lo:hi], in_=grouped[:]
                )

        def multiply(r, w_codes, w_scales):
            acc = acc_psum.tile([P, GROUP_COLS], F32, tag="acc")
            for lo, hi in PARTS:
                for g in range(PASSES):
                    nc.tensor.matmul_mx(
                        out=acc[:, lo:hi],
                        lhsT=x_codes[:, g, P * r : P * r + P].bitcast(FP8X4),
                        lhsT_scale=x_scales[:, g, P * r : P * r + P],
                        rhs=w_codes[:, g, lo:hi].bitcast(FP8X4),
                        rhs_scale=w_scales[:, g, lo:hi],
                        start=(g == 0),
                        stop=(g == PASSES - 1),
                    )
            return acc

        def multiply_by_table(r, acc):
            products = work.tile([P, 2, GROUP_HEADS, PAIRS, 2], F32, tag="products")
            shape = [P, GROUP_HEADS, PAIRS, 2, 2]
            nc.vector.tensor_tensor(
                out=products[:].rearrange("p w h n e -> p h n w e"),
                in0=acc[:].rearrange("p (h n w) -> p h n w", h=GROUP_HEADS, w=2).unsqueeze(4).to_broadcast(shape),
                in1=rot[:, r].unsqueeze(1).to_broadcast(shape),
                op=ALU.mult,
            )
            return products

        operands = {}
        finished = {}

        def prepare(group, half):
            if half == 0:
                w_codes = packed.tile([P, PASSES, GROUP_COLS], U32, tag="w_codes", align_bytes=64)
                w_scales = packed.tile([P, PASSES, GROUP_COLS], U8, tag="w_scales", align_bytes=64)
                operands[group] = (w_codes, w_scales)
            quantise_half(half, flip_half(group, half), *operands[group])

        def store(group):
            which, quarter = group
            first_head = quarter * GROUP_HEADS
            for b in range(BATCH):
                nc.sync.dma_start(
                    out=outputs[which][b, first_head : first_head + GROUP_HEADS].rearrange(
                        "h (m r) d -> m h (r d)", r=PHASES
                    ),
                    in_=finished[group][b:P:BATCH].rearrange("m h r d -> m h (r d)"),
                )

        for group, half in half_groups[:LEAD]:
            prepare(group, half)
        rot = const.tile([P, PHASES, PAIRS, 2, 2], F32)
        nc.scalar.activation(out=rot[:], in_=angle[:], func=ACT.Sin)

        for step in range(len(units) // 2):
            for group, half in half_groups[step + LEAD : step + LEAD + 1]:
                prepare(group, half)
            pair = units[2 * step : 2 * step + 2]
            accs = [multiply(r, *operands[group]) for group, r in pair]
            products = [
                multiply_by_table(r, acc) if group[0] != 2 else None for (group, r), acc in zip(pair, accs)
            ]
            for (group, r), acc, planes in zip(pair, accs, products):
                if r == 0:
                    result = results.tile([P, GROUP_HEADS, PHASES, HEAD_DIM], F32, tag="result")
                    finished[group] = result
                if planes is None:
                    nc.scalar.copy(
                        out=finished[group][:, :, r, :], in_=acc[:].rearrange("p (h d) -> p h d", h=GROUP_HEADS)
                    )
                else:
                    nc.gpsimd.tensor_tensor(
                        out=finished[group][:, :, r, :],
                        in0=planes[:, 0].rearrange("p h n e -> p h (n e)"),
                        in1=planes[:, 1].rearrange("p h n e -> p h (n e)"),
                        op=ALU.add,
                    )
                if r == PHASES - 1:
                    store(group)
